import numpy as np
import ml_dtypes


def mxq(x, axis, fmt="e4m3"):
    dtype, down = {"e4m3": (ml_dtypes.float8_e4m3fn, 7), "e5m2": (ml_dtypes.float8_e5m2, 14)}[fmt]
    v = np.moveaxis(np.asarray(x, np.float32).astype(ml_dtypes.bfloat16).astype(np.float64), axis, -1)
    blocks = v.reshape(v.shape[:-1] + (-1, 32))
    amax = np.abs(blocks).max(-1, keepdims=True)
    byte = np.maximum(np.where(amax > 0, np.frexp(amax)[1] - 1 + 127, 0) - down, 1)
    scale = np.exp2(byte - 127.0)
    codes = (blocks / scale).astype(np.float32).astype(dtype).astype(np.float64)
    return np.moveaxis((codes * scale).reshape(v.shape), -1, axis)


WIDE = False


def mx_kscale(k):
    if not WIDE:
        return np.ones(k)
    levels = np.array([10, -10, 5, -5, 0])
    a = np.random.permutation(np.resize(levels, k // 512 * 4)).reshape(k // 512, 4)
    idx = np.arange(k)
    return np.exp2(a[idx // 512, idx % 128 // 32])


BF16 = ml_dtypes.bfloat16


def bf(x):
    return np.asarray(x, np.float32).astype(BF16)


def f64(x):
    return np.asarray(x).astype(np.float64)


T, K, N = 1024, 2048, 2048


def _quantize(W, alpha_eff, bitwidth):
    Wa = W / alpha_eff
    Wc = np.clip(Wa, -1.0, 1.0)
    if bitwidth == 1:
        Q = np.sign(Wc)
        Q = np.where(Q == 0, 1.0, Q)
    elif bitwidth == 2:
        Q = np.where(np.abs(Wc) < 0.5, 0.0, np.sign(Wc))
    else:
        raise ValueError("bitwidth must be 1 or 2 here")
    return alpha_eff * Q


def setup_inputs():
    bound = 2.0 / np.sqrt(K)
    s = mx_kscale(K)
    g = np.maximum(s, 1.0) ** 2
    return {"x": bf(np.random.standard_normal((T, K)) * g[None, :]),
            "weight": bf(np.random.uniform(-bound, bound, (N, K)) / g[None, :]),
            "alpha": bf((1.5 / np.sqrt(K)) * (1.0 + 0.1 * np.random.standard_normal(1))),
            "bias": bf(0.1 * np.random.standard_normal(N)),
            "bitwidth": 2}


def reference(x, weight, alpha, bias, bitwidth):
    if bitwidth == 32:
        W_used = f64(weight)
    else:
        alpha_eff = np.abs(f64(alpha)) + 1e-8
        W_used = _quantize(f64(weight), alpha_eff, bitwidth)
    return (mxq(f64(x), 1, "e4m3") @ mxq(W_used, 1, "e4m3").T) + f64(bias)

@@ -1,0 +1,202 @@
+from contextlib import ExitStack
+
+import concourse.mybir as mybir
+from concourse.masks import make_identity
+
+FLOPS = 2 * 1024 * 2048 * 2048
+
+F32 = mybir.dt.float32
+BF16 = mybir.dt.bfloat16
+U32 = mybir.dt.uint32
+U8 = mybir.dt.uint8
+I32 = mybir.dt.int32
+FP8X4 = mybir.dt.float8_e4m3fn_x4
+ALU = mybir.AluOpType
+
+P = 128
+K = 2048
+UNIT = 256
+PASSES = 4
+GCOLS = 4 * UNIT
+
+
+def tile_quantizedlinear_kernel(tc, x, weight, alpha, bias, bitwidth, out):
+    assert bitwidth == 2
+    nc = tc.nc
+    with ExitStack() as ctx:
+        ctx.enter_context(tc.manual_schedule())
+        const = ctx.enter_context(tc.tile_pool(name="const", bufs=1))
+        nat = ctx.enter_context(tc.tile_pool(name="nat", bufs=4))
+        grp_pool = ctx.enter_context(tc.tile_pool(name="grp", bufs=4))
+        pos_pool = ctx.enter_context(tc.tile_pool(name="pos", bufs=2))
+        neg_pool = ctx.enter_context(tc.tile_pool(name="neg", bufs=2))
+        keep = ctx.enter_context(tc.tile_pool(name="keep", bufs=1))
+        stage = ctx.enter_context(tc.tile_pool(name="stage", bufs=6))
+        psum = ctx.enter_context(tc.psum_pool(name="psum", bufs=1))
+
+        def bank(b, name):
+            return psum.tile([P, 512], F32, tag="bank%d" % b, name=name)
+
+        raw = {}
+
+        def load(kind, u, parts=1):
+            src = weight if kind == "w" else x
+            t = nat.tile([P, 2 * K], BF16, tag="nat", name="%s_nat%d" % (kind, u))
+            raw[(kind, u)] = t
+            rows = src[u * UNIT:(u + 1) * UNIT, :].rearrange("(r p) k -> p r k", p=P)
+            dst = t[:].rearrange("p (r k) -> p r k", r=2)
+            w = K // parts
+            for q in range(parts):
+                nc.sync.dma_start(out=dst[:, :, q * w:(q + 1) * w], in_=rows[:, :, q * w:(q + 1) * w])
+
+        al = const.tile([P, 1], BF16, name="al")
+        nc.sync.dma_start(out=al[:], in_=alpha.partition_broadcast(P))
+        brow = const.tile([P, K], BF16, name="brow")
+        nc.vector.memset(brow[:].bitcast(I32), 0)
+        nc.scalar.dma_start(out=brow[0:1, :], in_=bias.rearrange("(o n) -> o n", o=1))
+        ones = const.tile([P, P], BF16, name="ones")
+        nc.vector.memset(ones[:], 1.0)
+        load("w", 0, parts=4)
+        load("w", 1)
+        load("x", 0)
+        load("x", 1)
+
+        ident = const.tile([P, P], F32, name="ident")
+        make_identity(nc, ident[:])
+
+        cst = const.tile([P, 4], F32, name="cst")
+        nc.vector.tensor_scalar(out=cst[:, 3:4], in0=al[:], scalar1=-1.0, scalar2=None, op0=ALU.mult)
+        nc.vector.tensor_tensor(out=cst[:, 3:4], in0=cst[:, 3:4], in1=al[:], op=ALU.max)
+        nc.vector.tensor_scalar(out=cst[:, 0:1], in0=cst[:, 3:4], scalar1=1e-8, scalar2=None, op0=ALU.add)
+        nc.vector.tensor_scalar(out=cst[:, 1:2], in0=cst[:, 3:4], scalar1=1e-8, scalar2=0.5, op0=ALU.add, op1=ALU.mult)
+        nc.vector.tensor_scalar(out=cst[:, 2:3], in0=cst[:, 3:4], scalar1=1e-8, scalar2=-0.5, op0=ALU.add, op1=ALU.mult)
+        a_col, t_col, nt_col = cst[:, 0:1], cst[:, 1:2], cst[:, 2:3]
+
+        grouped = {}
+
+        def transposes(kind, u):
+            words = raw[(kind, u)][:].bitcast(F32)
+            g_t = grp_pool.tile([P, 2 * K], BF16, tag="grp", name="grp_%s%d" % (kind, u), align_bytes=64)
+            grouped[(kind, u)] = g_t
+            g_w = g_t[:].bitcast(F32)
+            for g in range(PASSES):
+                bk = bank(g, "tr_%s%d_%d" % (kind, u, g))
+                view = bk[:].rearrange("p (r u j) -> p r u j", r=2, u=2)
+                for r in range(2):
+                    for h in range(2):
+                        c0 = r * (K // 2) + g * 256 + h * P
+                        nc.tensor.transpose(out=view[:, r, h, :], in_=words[:, c0:c0 + P], identity=ident[:])
+                nc.scalar.copy(
+                    out=g_w[:, g * 512:(g + 1) * 512].rearrange("p (r j u) -> p r j u", r=2, u=2),
+                    in_=bk[:].rearrange("p (r u j) -> p r j u", r=2, u=2),
+                )
+
+        tern = {}
+        negs = {}
+
+        def ternary(u, lo=0, hi=2 * K):
+            if u not in tern:
+                tern[u] = pos_pool.tile([P, 2 * K], BF16, tag="pos", name="pos%d" % u, align_bytes=64)
+                negs[u] = neg_pool.tile([P, 2 * K], BF16, tag="neg", name="neg%d" % u)
+            w = grouped[("w", u)][:, lo:hi]
+            nc.vector.tensor_scalar(out=tern[u][:, lo:hi], in0=w, scalar1=t_col, scalar2=a_col,
+                                    op0=ALU.is_ge, op1=ALU.mult)
+            nc.vector.tensor_scalar(out=negs[u][:, lo:hi], in0=w, scalar1=nt_col, scalar2=a_col,
+                                    op0=ALU.is_le, op1=ALU.mult)
+            nc.vector.tensor_tensor(out=tern[u][:, lo:hi], in0=tern[u][:, lo:hi], in1=negs[u][:, lo:hi],
+                                    op=ALU.subtract)
+
+        codes = {}
+        planes = {}
+
+        def quantise(kind, u):
+            c_t = keep.tile([P, 1024], U32, name="codes_%s%d" % (kind, u), align_bytes=64)
+            s_t = keep.tile([P, 1024], U8, name="plane_%s%d" % (kind, u), align_bytes=64)
+            codes[(kind, u)], planes[(kind, u)] = c_t, s_t
+            src = tern[u] if kind == "w" else grouped[("x", u)]
+            nc.vector.quantize_mx(out=c_t[:].bitcast(FP8X4), scales=s_t[:], in_=src[:])
+
+        acc = {}
+
+        def group(c, i, h, b=None):
+            if h == 0:
+                acc[(c, i)] = bank(b, "acc%d_%d" % (c, i))
+            xu, xo = i // 2, (i % 2) * P
+            wu = 2 * c + h
+            for g in range(PASSES):
+                nc.tensor.matmul_mx(
+                    out=acc[(c, i)][:, h * UNIT:(h + 1) * UNIT],
+                    lhsT=codes[("x", xu)][:, g * UNIT + xo:g * UNIT + xo + P].bitcast(FP8X4),
+                    lhsT_scale=planes[("x", xu)][:, g * UNIT + xo:g * UNIT + xo + P],
+                    rhs=codes[("w", wu)][:, g * UNIT:(g + 1) * UNIT].bitcast(FP8X4),
+                    rhs_scale=planes[("w", wu)][:, g * UNIT:(g + 1) * UNIT],
+                    start=(g == 0),
+                    stop=(g == PASSES - 1),
+                )
+
+        bias_sb = const.tile([P, K], F32, name="bias_sb")
+
+        def finish(c, i):
+            o = stage.tile([P, 512], F32, tag="o", name="o%d_%d" % (c, i))
+            nc.vector.tensor_tensor(out=o[:], in0=acc[(c, i)][:], in1=bias_sb[:, c * 512:(c + 1) * 512], op=ALU.add)
+            nc.sync.dma_start(out=out[i * P:(i + 1) * P, c * 512:(c + 1) * 512], in_=o[:])
+
+        def mx_half(hc):
+            c, i0 = hc // 2, 4 * (hc % 2)
+            for i in range(i0, i0 + 4):
+                group(c, i, 0, 4 + i % 4)
+            for i in range(i0, i0 + 4):
+                group(c, i, 1)
+
+        def finish_half(hc):
+            c, i0 = hc // 2, 4 * (hc % 2)
+            for i in range(i0, i0 + 4):
+                finish(c, i)
+
+        transposes("w", 0)
+        load("w", 2)
+        for g in range(PASSES):
+            ternary(0, g * GCOLS, (g + 1) * GCOLS)
+        transposes("w", 1)
+        load("x", 2)
+        transposes("x", 0)
+        load("x", 3)
+        transposes("x", 1)
+        load("w", 3)
+        ternary(1)
+        transposes("w", 2)
+        load("w", 4)
+        quantise("w", 0)
+        for b in range(4):
+            bk = bank(4 + b, "bias_bk%d" % b)
+            nc.tensor.matmul(out=bk[:], lhsT=ones[:], rhs=brow[:, b * 512:(b + 1) * 512], start=True, stop=True)
+            nc.scalar.copy(out=bias_sb[:, b * 512:(b + 1) * 512], in_=bk[:])
+        transposes("x", 2)
+        load("w", 5)
+        quantise("x", 0)
+        quantise("x", 1)
+        quantise("w", 1)
+        mx_half(0)
+        transposes("x", 3)
+        load("w", 6)
+        transposes("w", 3)
+        load("w", 7)
+        for j in range(2, 8):
+            ternary(j)
+            if j + 2 < 8:
+                transposes("w", j + 2)
+            finish_half(j - 2)
+            quantise("w", j)
+            if j == 2:
+                quantise("x", 2)
+                quantise("x", 3)
+            if j < 7:
+                mx_half(j - 1)
+            if j == 6:
+                for i in (4, 5, 6, 7):
+                    group(3, i, 0, i % 4)
+        for i in (0, 1, 2, 3):
+            group(3, i, 0, 4 + i)
+        for i in (4, 5, 6, 7, 0, 1, 2, 3):
+            group(3, i, 1)
+            finish(3, i)

@@ -12,12 +12,14 @@ U8 = mybir.dt.uint8
 I32 = mybir.dt.int32
 FP8X4 = mybir.dt.float8_e4m3fn_x4
 ALU = mybir.AluOpType
+ACT = mybir.ActivationFunctionType
 
 P = 128
 K = 2048
 UNIT = 256
 PASSES = 4
 GCOLS = 4 * UNIT
+S_PATH = (3, 4, 5)
 
 
 def tile_quantizedlinear_kernel(tc, x, weight, alpha, bias, bitwidth, out):
@@ -26,12 +28,13 @@ def tile_quantizedlinear_kernel(tc, x, weight, alpha, bias, bitwidth, out):
     with ExitStack() as ctx:
         ctx.enter_context(tc.manual_schedule())
         const = ctx.enter_context(tc.tile_pool(name="const", bufs=1))
-        nat = ctx.enter_context(tc.tile_pool(name="nat", bufs=4))
-        grp_pool = ctx.enter_context(tc.tile_pool(name="grp", bufs=4))
+        nat = ctx.enter_context(tc.tile_pool(name="nat", bufs=3))
+        grp_pool = ctx.enter_context(tc.tile_pool(name="grp", bufs=8))
         pos_pool = ctx.enter_context(tc.tile_pool(name="pos", bufs=2))
         neg_pool = ctx.enter_context(tc.tile_pool(name="neg", bufs=2))
         keep = ctx.enter_context(tc.tile_pool(name="keep", bufs=1))
         stage = ctx.enter_context(tc.tile_pool(name="stage", bufs=6))
+        flip = ctx.enter_context(tc.tile_pool(name="flip", bufs=4))
         psum = ctx.enter_context(tc.psum_pool(name="psum", bufs=1))
 
         def bank(b, name):
@@ -56,10 +59,18 @@ def tile_quantizedlinear_kernel(tc, x, weight, alpha, bias, bitwidth, out):
         nc.scalar.dma_start(out=brow[0:1, :], in_=bias.rearrange("(o n) -> o n", o=1))
         ones = const.tile([P, P], BF16, name="ones")
         nc.vector.memset(ones[:], 1.0)
-        load("w", 0, parts=4)
-        load("w", 1)
-        load("x", 0)
-        load("x", 1)
+
+        units = [("w", 0), ("x", 0), ("x", 1), ("w", 1), ("x", 2), ("x", 3)] + [("w", u) for u in range(2, 8)]
+        loaded = [0]
+
+        def load_next():
+            if loaded[0] < len(units):
+                kind, u = units[loaded[0]]
+                load(kind, u, parts=4 if loaded[0] == 0 else 1)
+                loaded[0] += 1
+
+        for q in range(3):
+            load_next()
 
         ident = const.tile([P, P], F32, name="ident")
         make_identity(nc, ident[:])
@@ -90,21 +101,32 @@ def tile_quantizedlinear_kernel(tc, x, weight, alpha, bias, bitwidth, out):
                     out=g_w[:, g * 512:(g + 1) * 512].rearrange("p (r j u) -> p r j u", r=2, u=2),
                     in_=bk[:].rearrange("p (r u j) -> p r j u", r=2, u=2),
                 )
+            load_next()
 
         tern = {}
         negs = {}
 
-        def ternary(u, lo=0, hi=2 * K):
+        def t_pos(u, lo=0, hi=2 * K):
             if u not in tern:
                 tern[u] = pos_pool.tile([P, 2 * K], BF16, tag="pos", name="pos%d" % u, align_bytes=64)
                 negs[u] = neg_pool.tile([P, 2 * K], BF16, tag="neg", name="neg%d" % u)
-            w = grouped[("w", u)][:, lo:hi]
-            nc.vector.tensor_scalar(out=tern[u][:, lo:hi], in0=w, scalar1=t_col, scalar2=a_col,
-                                    op0=ALU.is_ge, op1=ALU.mult)
-            nc.vector.tensor_scalar(out=negs[u][:, lo:hi], in0=w, scalar1=nt_col, scalar2=a_col,
-                                    op0=ALU.is_le, op1=ALU.mult)
+            nc.vector.tensor_scalar(out=tern[u][:, lo:hi], in0=grouped[("w", u)][:, lo:hi], scalar1=t_col,
+                                    scalar2=a_col, op0=ALU.is_ge, op1=ALU.mult)
+
+        def t_neg(u, lo=0, hi=2 * K):
+            nc.vector.tensor_scalar(out=negs[u][:, lo:hi], in0=grouped[("w", u)][:, lo:hi], scalar1=nt_col,
+                                    scalar2=a_col, op0=ALU.is_le, op1=ALU.mult)
+
+        def t_sub(u, lo=0, hi=2 * K):
             nc.vector.tensor_tensor(out=tern[u][:, lo:hi], in0=tern[u][:, lo:hi], in1=negs[u][:, lo:hi],
                                     op=ALU.subtract)
+
+        def ternary(u, parts=1):
+            n = 2 * K // parts
+            for q in range(parts):
+                t_pos(u, q * n, (q + 1) * n)
+                t_neg(u, q * n, (q + 1) * n)
+                t_sub(u, q * n, (q + 1) * n)
 
         codes = {}
         planes = {}
@@ -116,87 +138,136 @@ def tile_quantizedlinear_kernel(tc, x, weight, alpha, bias, bitwidth, out):
             src = tern[u] if kind == "w" else grouped[("x", u)]
             nc.vector.quantize_mx(out=c_t[:].bitcast(FP8X4), scales=s_t[:], in_=src[:])
 
-        acc = {}
-
-        def group(c, i, h, b=None):
-            if h == 0:
-                acc[(c, i)] = bank(b, "acc%d_%d" % (c, i))
-            xu, xo = i // 2, (i % 2) * P
-            wu = 2 * c + h
+        def passes(dst, stat, s0, mov):
             for g in range(PASSES):
                 nc.tensor.matmul_mx(
-                    out=acc[(c, i)][:, h * UNIT:(h + 1) * UNIT],
-                    lhsT=codes[("x", xu)][:, g * UNIT + xo:g * UNIT + xo + P].bitcast(FP8X4),
-                    lhsT_scale=planes[("x", xu)][:, g * UNIT + xo:g * UNIT + xo + P],
-                    rhs=codes[("w", wu)][:, g * UNIT:(g + 1) * UNIT].bitcast(FP8X4),
-                    rhs_scale=planes[("w", wu)][:, g * UNIT:(g + 1) * UNIT],
+                    out=dst,
+                    lhsT=codes[stat][:, g * UNIT + s0:g * UNIT + s0 + P].bitcast(FP8X4),
+                    lhsT_scale=planes[stat][:, g * UNIT + s0:g * UNIT + s0 + P],
+                    rhs=codes[mov][:, g * UNIT:(g + 1) * UNIT].bitcast(FP8X4),
+                    rhs_scale=planes[mov][:, g * UNIT:(g + 1) * UNIT],
                     start=(g == 0),
                     stop=(g == PASSES - 1),
                 )
 
         bias_sb = const.tile([P, K], F32, name="bias_sb")
+        bias_col = const.tile([P, 16], F32, name="bias_col")
 
-        def finish(c, i):
-            o = stage.tile([P, 512], F32, tag="o", name="o%d_%d" % (c, i))
-            nc.vector.tensor_tensor(out=o[:], in0=acc[(c, i)][:], in1=bias_sb[:, c * 512:(c + 1) * 512], op=ALU.add)
-            nc.sync.dma_start(out=out[i * P:(i + 1) * P, c * 512:(c + 1) * 512], in_=o[:])
+        def bias_rows(bs):
+            for b in bs:
+                bk = bank(6 + b % 2, "bias_bk%d" % b)
+                nc.tensor.matmul(out=bk[:], lhsT=ones[:], rhs=brow[:, b * 512:(b + 1) * 512], start=True, stop=True)
+                nc.scalar.copy(out=bias_sb[:, b * 512:(b + 1) * 512], in_=bk[:])
 
-        def mx_half(hc):
-            c, i0 = hc // 2, 4 * (hc % 2)
-            for i in range(i0, i0 + 4):
-                group(c, i, 0, 4 + i % 4)
-            for i in range(i0, i0 + 4):
-                group(c, i, 1)
+        def bias_columns(base):
+            tiles = [2 * u + a for u in S_PATH for a in range(2)]
+            for b in range((len(tiles) + 3) // 4):
+                part = tiles[4 * b:4 * b + 4]
+                bk = bank(base + b, "bcol_bk%d" % b)
+                for q, nt in enumerate(part):
+                    nc.tensor.transpose(out=bk[:, q * P:(q + 1) * P], in_=bias_sb[:, nt * P:(nt + 1) * P],
+                                        identity=ident[:])
+                nc.scalar.copy(out=bias_col[:, part[0]:part[0] + len(part)],
+                               in_=bk[:].rearrange("p (q j) -> p q j", q=4)[:, 0:len(part), 0])
 
-        def finish_half(hc):
-            c, i0 = hc // 2, 4 * (hc % 2)
-            for i in range(i0, i0 + 4):
-                finish(c, i)
+        acc = {}
+
+        def store(u, q, o):
+            nc.sync.dma_start(
+                out=out[q * UNIT:(q + 1) * UNIT, u * UNIT:(u + 1) * UNIT].rearrange("(h p) n -> p h n", p=P),
+                in_=o[:].rearrange("p (h n) -> p h n", h=2),
+            )
+
+        def mx_v(u, base, qs=(0, 1, 2, 3)):
+            for q in qs:
+                acc[(u, q)] = bank(base + q, "acc%d_%d" % (u, q))
+                for h in range(2):
+                    passes(acc[(u, q)][:, h * UNIT:(h + 1) * UNIT], ("x", q), h * P, ("w", u))
+
+        def finish_v(u, qs=(0, 1, 2, 3)):
+            for q in qs:
+                o = stage.tile([P, 512], F32, tag="o", name="o%d_%d" % (u, q))
+                nc.vector.tensor_tensor(
+                    out=o[:].rearrange("p (h n) -> p h n", h=2),
+                    in0=acc[(u, q)][:].rearrange("p (h n) -> p h n", h=2),
+                    in1=bias_sb[:, u * UNIT:(u + 1) * UNIT].unsqueeze(1).to_broadcast([P, 2, UNIT]),
+                    op=ALU.add,
+                )
+                store(u, q, o)
+
+        def mx_s(u, base):
+            flipped = {}
+            for b in range(2):
+                for a in range(2):
+                    bk = bank(base + 2 * b + a, "accT%d_%d%d" % (u, b, a))
+                    for h in range(2):
+                        passes(bk[:, h * UNIT:(h + 1) * UNIT], ("w", u), a * P, ("x", 2 * b + h))
+                    f = flip.tile([P, 512], F32, tag="f", name="f%d_%d%d" % (u, b, a))
+                    flipped[(b, a)] = f
+                    nc.scalar.activation(out=f[:], in_=bk[:], func=ACT.Identity,
+                                         bias=bias_col[:, 2 * u + a:2 * u + a + 1], scale=1.0)
+            for q in range(4):
+                bk = bank(base + q, "back%d_%d" % (u, q))
+                for h in range(2):
+                    for a in range(2):
+                        c0 = (q % 2) * UNIT + h * P
+                        nc.tensor.transpose(out=bk[:, h * UNIT + a * P:h * UNIT + (a + 1) * P],
+                                            in_=flipped[(q // 2, a)][:, c0:c0 + P], identity=ident[:])
+                o = stage.tile([P, 512], F32, tag="o", name="o%d_%d" % (u, q))
+                nc.scalar.copy(out=o[:], in_=bk[:])
+                store(u, q, o)
 
         transposes("w", 0)
-        load("w", 2)
-        for g in range(PASSES):
-            ternary(0, g * GCOLS, (g + 1) * GCOLS)
-        transposes("w", 1)
-        load("x", 2)
         transposes("x", 0)
-        load("x", 3)
         transposes("x", 1)
-        load("w", 3)
-        ternary(1)
-        transposes("w", 2)
-        load("w", 4)
+        ternary(0, parts=4)
         quantise("w", 0)
-        for b in range(4):
-            bk = bank(4 + b, "bias_bk%d" % b)
-            nc.tensor.matmul(out=bk[:], lhsT=ones[:], rhs=brow[:, b * 512:(b + 1) * 512], start=True, stop=True)
-            nc.scalar.copy(out=bias_sb[:, b * 512:(b + 1) * 512], in_=bk[:])
-        transposes("x", 2)
-        load("w", 5)
+        transposes("w", 1)
         quantise("x", 0)
         quantise("x", 1)
-        quantise("w", 1)
-        mx_half(0)
+        mx_v(0, 4, (0, 1))
+        bias_rows((0, 1))
+        transposes("x", 2)
         transposes("x", 3)
-        load("w", 6)
+        ternary(1, parts=2)
+        quantise("w", 1)
+        mx_v(1, 6, (0, 1))
+        transposes("w", 2)
+        finish_v(0, (0, 1))
+        quantise("x", 2)
+        quantise("x", 3)
+        mx_v(0, 2, (2, 3))
         transposes("w", 3)
-        load("w", 7)
-        for j in range(2, 8):
-            ternary(j)
-            if j + 2 < 8:
-                transposes("w", j + 2)
-            finish_half(j - 2)
-            quantise("w", j)
-            if j == 2:
-                quantise("x", 2)
-                quantise("x", 3)
+        finish_v(1, (0, 1))
+        mx_v(1, 4, (2, 3))
+        transposes("w", 4)
+        ternary(2, parts=2)
+        finish_v(0, (2, 3))
+        quantise("w", 2)
+        mx_v(2, 4, (0, 1))
+        transposes("w", 5)
+        finish_v(1, (2, 3))
+        bias_rows((2, 3))
+        mx_v(2, 4, (2, 3))
+        transposes("w", 6)
+        ternary(3)
+        finish_v(2, (0, 1))
+        quantise("w", 3)
+        transposes("w", 7)
+        bias_columns(4)
+        finish_v(2, (2, 3))
+        mx_s(3, 0)
+        t_pos(4)
+        for j in range(4, 8):
+            t_neg(j)
+            t_sub(j)
             if j < 7:
-                mx_half(j - 1)
-            if j == 6:
-                for i in (4, 5, 6, 7):
-                    group(3, i, 0, i % 4)
-        for i in (0, 1, 2, 3):
-            group(3, i, 0, 4 + i)
-        for i in (4, 5, 6, 7, 0, 1, 2, 3):
-            group(3, i, 1)
-            finish(3, i)
+                t_pos(j + 1)
+            quantise("w", j)
+            base = 4 if j % 2 == 0 else 0
+            if j in S_PATH:
+                mx_s(j, base)
+            else:
+                mx_v(j, base)
+        finish_v(6)
+        finish_v(7)

from contextlib import ExitStack

import concourse.mybir as mybir
from concourse.masks import make_identity

FLOPS = 2 * 1024 * 2048 * 2048

F32 = mybir.dt.float32
BF16 = mybir.dt.bfloat16
U32 = mybir.dt.uint32
U8 = mybir.dt.uint8
I32 = mybir.dt.int32
FP8X4 = mybir.dt.float8_e4m3fn_x4
ALU = mybir.AluOpType
ACT = mybir.ActivationFunctionType

P = 128
K = 2048
UNIT = 256
PASSES = 4
GCOLS = 4 * UNIT
S_PATH = (3, 4, 5)


def tile_quantizedlinear_kernel(tc, x, weight, alpha, bias, bitwidth, out):
    assert bitwidth == 2
    nc = tc.nc
    with ExitStack() as ctx:
        ctx.enter_context(tc.manual_schedule())
        const = ctx.enter_context(tc.tile_pool(name="const", bufs=1))
        nat = ctx.enter_context(tc.tile_pool(name="nat", bufs=3))
        grp_pool = ctx.enter_context(tc.tile_pool(name="grp", bufs=8))
        pos_pool = ctx.enter_context(tc.tile_pool(name="pos", bufs=2))
        neg_pool = ctx.enter_context(tc.tile_pool(name="neg", bufs=2))
        keep = ctx.enter_context(tc.tile_pool(name="keep", bufs=1))
        stage = ctx.enter_context(tc.tile_pool(name="stage", bufs=6))
        flip = ctx.enter_context(tc.tile_pool(name="flip", bufs=4))
        psum = ctx.enter_context(tc.psum_pool(name="psum", bufs=1))

        def bank(b, name):
            return psum.tile([P, 512], F32, tag="bank%d" % b, name=name)

        raw = {}

        def load(kind, u, parts=1):
            src = weight if kind == "w" else x
            t = nat.tile([P, 2 * K], BF16, tag="nat", name="%s_nat%d" % (kind, u))
            raw[(kind, u)] = t
            rows = src[u * UNIT:(u + 1) * UNIT, :].rearrange("(r p) k -> p r k", p=P)
            dst = t[:].rearrange("p (r k) -> p r k", r=2)
            w = K // parts
            for q in range(parts):
                nc.sync.dma_start(out=dst[:, :, q * w:(q + 1) * w], in_=rows[:, :, q * w:(q + 1) * w])

        al = const.tile([P, 1], BF16, name="al")
        nc.sync.dma_start(out=al[:], in_=alpha.partition_broadcast(P))
        brow = const.tile([P, K], BF16, name="brow")
        nc.vector.memset(brow[:].bitcast(I32), 0)
        nc.scalar.dma_start(out=brow[0:1, :], in_=bias.rearrange("(o n) -> o n", o=1))
        ones = const.tile([P, P], BF16, name="ones")
        nc.vector.memset(ones[:], 1.0)

        units = [("w", 0), ("x", 0), ("x", 1), ("w", 1), ("x", 2), ("x", 3)] + [("w", u) for u in range(2, 8)]
        loaded = [0]

        def load_next():
            if loaded[0] < len(units):
                kind, u = units[loaded[0]]
                load(kind, u, parts=4 if loaded[0] == 0 else 1)
                loaded[0] += 1

        for q in range(3):
            load_next()

        ident = const.tile([P, P], F32, name="ident")
        make_identity(nc, ident[:])

        cst = const.tile([P, 4], F32, name="cst")
        nc.vector.tensor_scalar(out=cst[:, 3:4], in0=al[:], scalar1=-1.0, scalar2=None, op0=ALU.mult)
        nc.vector.tensor_tensor(out=cst[:, 3:4], in0=cst[:, 3:4], in1=al[:], op=ALU.max)
        nc.vector.tensor_scalar(out=cst[:, 0:1], in0=cst[:, 3:4], scalar1=1e-8, scalar2=None, op0=ALU.add)
        nc.vector.tensor_scalar(out=cst[:, 1:2], in0=cst[:, 3:4], scalar1=1e-8, scalar2=0.5, op0=ALU.add, op1=ALU.mult)
        nc.vector.tensor_scalar(out=cst[:, 2:3], in0=cst[:, 3:4], scalar1=1e-8, scalar2=-0.5, op0=ALU.add, op1=ALU.mult)
        a_col, t_col, nt_col = cst[:, 0:1], cst[:, 1:2], cst[:, 2:3]

        grouped = {}

        def transposes(kind, u):
            words = raw[(kind, u)][:].bitcast(F32)
            g_t = grp_pool.tile([P, 2 * K], BF16, tag="grp", name="grp_%s%d" % (kind, u), align_bytes=64)
            grouped[(kind, u)] = g_t
            g_w = g_t[:].bitcast(F32)
            for g in range(PASSES):
                bk = bank(g, "tr_%s%d_%d" % (kind, u, g))
                view = bk[:].rearrange("p (r u j) -> p r u j", r=2, u=2)
                for r in range(2):
                    for h in range(2):
                        c0 = r * (K // 2) + g * 256 + h * P
                        nc.tensor.transpose(out=view[:, r, h, :], in_=words[:, c0:c0 + P], identity=ident[:])
                nc.scalar.copy(
                    out=g_w[:, g * 512:(g + 1) * 512].rearrange("p (r j u) -> p r j u", r=2, u=2),
                    in_=bk[:].rearrange("p (r u j) -> p r j u", r=2, u=2),
                )
            load_next()

        tern = {}
        negs = {}

        def t_pos(u, lo=0, hi=2 * K):
            if u not in tern:
                tern[u] = pos_pool.tile([P, 2 * K], BF16, tag="pos", name="pos%d" % u, align_bytes=64)
                negs[u] = neg_pool.tile([P, 2 * K], BF16, tag="neg", name="neg%d" % u)
            nc.vector.tensor_scalar(out=tern[u][:, lo:hi], in0=grouped[("w", u)][:, lo:hi], scalar1=t_col,
                                    scalar2=a_col, op0=ALU.is_ge, op1=ALU.mult)

        def t_neg(u, lo=0, hi=2 * K):
            nc.vector.tensor_scalar(out=negs[u][:, lo:hi], in0=grouped[("w", u)][:, lo:hi], scalar1=nt_col,
                                    scalar2=a_col, op0=ALU.is_le, op1=ALU.mult)

        def t_sub(u, lo=0, hi=2 * K):
            nc.vector.tensor_tensor(out=tern[u][:, lo:hi], in0=tern[u][:, lo:hi], in1=negs[u][:, lo:hi],
                                    op=ALU.subtract)

        def ternary(u, parts=1):
            n = 2 * K // parts
            for q in range(parts):
                t_pos(u, q * n, (q + 1) * n)
                t_neg(u, q * n, (q + 1) * n)
                t_sub(u, q * n, (q + 1) * n)

        codes = {}
        planes = {}

        def quantise(kind, u):
            c_t = keep.tile([P, 1024], U32, name="codes_%s%d" % (kind, u), align_bytes=64)
            s_t = keep.tile([P, 1024], U8, name="plane_%s%d" % (kind, u), align_bytes=64)
            codes[(kind, u)], planes[(kind, u)] = c_t, s_t
            src = tern[u] if kind == "w" else grouped[("x", u)]
            nc.vector.quantize_mx(out=c_t[:].bitcast(FP8X4), scales=s_t[:], in_=src[:])

        def passes(dst, stat, s0, mov):
            for g in range(PASSES):
                nc.tensor.matmul_mx(
                    out=dst,
                    lhsT=codes[stat][:, g * UNIT + s0:g * UNIT + s0 + P].bitcast(FP8X4),
                    lhsT_scale=planes[stat][:, g * UNIT + s0:g * UNIT + s0 + P],
                    rhs=codes[mov][:, g * UNIT:(g + 1) * UNIT].bitcast(FP8X4),
                    rhs_scale=planes[mov][:, g * UNIT:(g + 1) * UNIT],
                    start=(g == 0),
                    stop=(g == PASSES - 1),
                )

        bias_sb = const.tile([P, K], F32, name="bias_sb")
        bias_col = const.tile([P, 16], F32, name="bias_col")

        def bias_rows(bs):
            for b in bs:
                bk = bank(6 + b % 2, "bias_bk%d" % b)
                nc.tensor.matmul(out=bk[:], lhsT=ones[:], rhs=brow[:, b * 512:(b + 1) * 512], start=True, stop=True)
                nc.scalar.copy(out=bias_sb[:, b * 512:(b + 1) * 512], in_=bk[:])

        def bias_columns(base):
            tiles = [2 * u + a for u in S_PATH for a in range(2)]
            for b in range((len(tiles) + 3) // 4):
                part = tiles[4 * b:4 * b + 4]
                bk = bank(base + b, "bcol_bk%d" % b)
                for q, nt in enumerate(part):
                    nc.tensor.transpose(out=bk[:, q * P:(q + 1) * P], in_=bias_sb[:, nt * P:(nt + 1) * P],
                                        identity=ident[:])
                nc.scalar.copy(out=bias_col[:, part[0]:part[0] + len(part)],
                               in_=bk[:].rearrange("p (q j) -> p q j", q=4)[:, 0:len(part), 0])

        acc = {}

        def store(u, q, o):
            nc.sync.dma_start(
                out=out[q * UNIT:(q + 1) * UNIT, u * UNIT:(u + 1) * UNIT].rearrange("(h p) n -> p h n", p=P),
                in_=o[:].rearrange("p (h n) -> p h n", h=2),
            )

        def mx_v(u, base, qs=(0, 1, 2, 3)):
            for q in qs:
                acc[(u, q)] = bank(base + q, "acc%d_%d" % (u, q))
                for h in range(2):
                    passes(acc[(u, q)][:, h * UNIT:(h + 1) * UNIT], ("x", q), h * P, ("w", u))

        def finish_v(u, qs=(0, 1, 2, 3)):
            for q in qs:
                o = stage.tile([P, 512], F32, tag="o", name="o%d_%d" % (u, q))
                nc.vector.tensor_tensor(
                    out=o[:].rearrange("p (h n) -> p h n", h=2),
                    in0=acc[(u, q)][:].rearrange("p (h n) -> p h n", h=2),
                    in1=bias_sb[:, u * UNIT:(u + 1) * UNIT].unsqueeze(1).to_broadcast([P, 2, UNIT]),
                    op=ALU.add,
                )
                store(u, q, o)

        def mx_s(u, base):
            flipped = {}
            for b in range(2):
                for a in range(2):
                    bk = bank(base + 2 * b + a, "accT%d_%d%d" % (u, b, a))
                    for h in range(2):
                        passes(bk[:, h * UNIT:(h + 1) * UNIT], ("w", u), a * P, ("x", 2 * b + h))
                    f = flip.tile([P, 512], F32, tag="f", name="f%d_%d%d" % (u, b, a))
                    flipped[(b, a)] = f
                    nc.scalar.activation(out=f[:], in_=bk[:], func=ACT.Identity,
                                         bias=bias_col[:, 2 * u + a:2 * u + a + 1], scale=1.0)
            for q in range(4):
                bk = bank(base + q, "back%d_%d" % (u, q))
                for h in range(2):
                    for a in range(2):
                        c0 = (q % 2) * UNIT + h * P
                        nc.tensor.transpose(out=bk[:, h * UNIT + a * P:h * UNIT + (a + 1) * P],
                                            in_=flipped[(q // 2, a)][:, c0:c0 + P], identity=ident[:])
                o = stage.tile([P, 512], F32, tag="o", name="o%d_%d" % (u, q))
                nc.scalar.copy(out=o[:], in_=bk[:])
                store(u, q, o)

        transposes("w", 0)
        transposes("x", 0)
        transposes("x", 1)
        ternary(0, parts=4)
        quantise("w", 0)
        transposes("w", 1)
        quantise("x", 0)
        quantise("x", 1)
        mx_v(0, 4, (0, 1))
        bias_rows((0, 1))
        transposes("x", 2)
        transposes("x", 3)
        ternary(1, parts=2)
        quantise("w", 1)
        mx_v(1, 6, (0, 1))
        transposes("w", 2)
        finish_v(0, (0, 1))
        quantise("x", 2)
        quantise("x", 3)
        mx_v(0, 2, (2, 3))
        transposes("w", 3)
        finish_v(1, (0, 1))
        mx_v(1, 4, (2, 3))
        transposes("w", 4)
        ternary(2, parts=2)
        finish_v(0, (2, 3))
        quantise("w", 2)
        mx_v(2, 4, (0, 1))
        transposes("w", 5)
        finish_v(1, (2, 3))
        bias_rows((2, 3))
        mx_v(2, 4, (2, 3))
        transposes("w", 6)
        ternary(3)
        finish_v(2, (0, 1))
        quantise("w", 3)
        transposes("w", 7)
        bias_columns(4)
        finish_v(2, (2, 3))
        mx_s(3, 0)
        t_pos(4)
        for j in range(4, 8):
            t_neg(j)
            t_sub(j)
            if j < 7:
                t_pos(j + 1)
            quantise("w", j)
            base = 4 if j % 2 == 0 else 0
            if j in S_PATH:
                mx_s(j, base)
            else:
                mx_v(j, base)
        finish_v(6)
        finish_v(7)
